import numpy as np
import ml_dtypes


def mxq(x, axis, fmt="e4m3"):
    dtype, down = {"e4m3": (ml_dtypes.float8_e4m3fn, 7), "e5m2": (ml_dtypes.float8_e5m2, 14)}[fmt]
    v = np.moveaxis(np.asarray(x, np.float32).astype(ml_dtypes.bfloat16).astype(np.float64), axis, -1)
    blocks = v.reshape(v.shape[:-1] + (-1, 32))
    amax = np.abs(blocks).max(-1, keepdims=True)
    byte = np.maximum(np.where(amax > 0, np.frexp(amax)[1] - 1 + 127, 0) - down, 1)
    scale = np.exp2(byte - 127.0)
    codes = (blocks / scale).astype(np.float32).astype(dtype).astype(np.float64)
    return np.moveaxis((codes * scale).reshape(v.shape), -1, axis)


WIDE = False


def mx_kscale(k):
    if not WIDE:
        return np.ones(k)
    levels = np.array([10, -10, 5, -5, 0])
    if k % 512:
        return np.exp2(np.random.permutation(np.resize(levels, k // 32))).repeat(32)
    a = np.empty((k // 512, 16))
    for p in range(k // 512):
        a[p, :8] = np.random.permutation(np.resize(levels, 8))
        for g in range(8):
            far = levels[np.abs(levels - a[p, g]) >= 10]
            a[p, g + 8] = far[np.random.randint(len(far))]
    return np.exp2(a.ravel()).repeat(32)


BF16 = ml_dtypes.bfloat16


def bf(x):
    return np.asarray(x, np.float32).astype(BF16)


def f64(x):
    return np.asarray(x).astype(np.float64)


B, T, KA, KT, DIM, NH, HD, E = 2, 512, 256, 256, 1024, 8, 128, 8
ROPE_BASE = 10000.0


def rope_cos_sin(L, hd):
    inv_freq = 1.0 / (ROPE_BASE ** (f64(np.arange(0, hd, 2)) / hd))
    freqs = f64(np.arange(L))[:, None] * inv_freq[None, :]
    emb = np.concatenate([freqs, freqs], axis=-1)
    return np.cos(emb), np.sin(emb)


def rotate_half(x):
    x1 = x[..., 0::2]
    x2 = x[..., 1::2]
    return np.stack((-x2, x1), axis=-1).reshape(x.shape)


def rope(t, cos, sin):
    return t * cos[None, None] + rotate_half(t) * sin[None, None]


def heads(t):
    return t.reshape(B, -1, NH, HD).transpose(0, 2, 1, 3)


def draw0():
    s = mx_kscale(DIM)
    c = 1.2 / np.sqrt(DIM)
    return {"x": bf(np.random.standard_normal((B, T, DIM)) * s),
            "W_qa": bf(np.random.standard_normal((NH * HD, DIM)) * c / s[None, :]),
            "b_qa": bf(np.random.standard_normal(NH * HD) * 0.3),
            "W_qt": bf(np.random.standard_normal((NH * HD, DIM)) * c / s[None, :]),
            "b_qt": bf(np.random.standard_normal(NH * HD) * 0.3)}


def core(x, W_qa, b_qa, W_qt, b_qt):
    xq = mxq(f64(x), 2, "e4m3")
    q_a = heads((xq @ mxq(f64(W_qa), 1, "e4m3").T) + f64(b_qa))
    q_t = heads((xq @ mxq(f64(W_qt), 1, "e4m3").T) + f64(b_qt))
    cos_m, sin_m = rope_cos_sin(T, HD)
    return rope(q_a, cos_m, sin_m), rope(q_t, cos_m, sin_m)


def e4m3fn_bytes(y):
    return np.clip(np.asarray(y, np.float64), -448.0, 448.0).astype(np.float32).astype(ml_dtypes.float8_e4m3fn).view(np.uint8)


def e4m3fn_values(b):
    return np.asarray(b, np.uint8).view(ml_dtypes.float8_e4m3fn).astype(np.float64)


def setup_inputs():
    d = draw0()
    x0 = np.asarray(d['x']).astype(np.float64)
    s = (np.max(np.abs(x0), axis=(0, 1), keepdims=True) / 448.0).astype(np.float32)
    out = {}
    for k, v in d.items():
        if k == 'x':
            out['x_bytes'] = e4m3fn_bytes(x0 / s.astype(np.float64))
            out['x_scale'] = s
        else:
            out[k] = v
    return out


def reference(x_bytes, x_scale, W_qa, b_qa, W_qt, b_qt):
    return core(e4m3fn_values(x_bytes) * x_scale.astype(np.float64), W_qa, b_qa, W_qt, b_qt)

@@ -1,0 +1,308 @@
+from contextlib import ExitStack
+import math
+
+import concourse.mybir as mybir
+from concourse.masks import make_identity
+
+F32 = mybir.dt.float32
+BF16 = mybir.dt.bfloat16
+U8 = mybir.dt.uint8
+U32 = mybir.dt.uint32
+I32 = mybir.dt.int32
+FP8 = mybir.dt.float8_e4m3fn
+FP8X4 = mybir.dt.float8_e4m3fn_x4
+ALU = mybir.AluOpType
+ACT = mybir.ActivationFunctionType
+
+B, T, DIM, NH, HD = 2, 512, 1024, 8, 128
+P = 128
+ROPE_BASE = 10000.0
+FLOPS = 2 * (B * T) * DIM * (2 * NH * HD)
+
+TWO_PI = 2.0 * math.pi
+C1 = 6.28125
+C2 = TWO_PI - C1
+KINDS = (1, 6, 2) * 10 + (1, 6)
+
+
+def tile_l1regressionmoeactionhead_pa_kernel(tc, x_bytes, x_scale, W_qa, b_qa, W_qt, b_qt, out_0, out_1):
+    nc = tc.nc
+    outs = (out_0, out_1)
+    weights = (W_qa, W_qt)
+
+    with ExitStack() as ctx:
+        const = ctx.enter_context(tc.tile_pool(name="const", bufs=1))
+        raw = ctx.enter_context(tc.tile_pool(name="raw", bufs=1))
+        keep = ctx.enter_context(tc.tile_pool(name="keep", bufs=1))
+        stage = ctx.enter_context(tc.tile_pool(name="stage", bufs=8))
+        epi = ctx.enter_context(tc.tile_pool(name="epi", bufs=4))
+        ps_acc = ctx.enter_context(tc.psum_pool(name="ps_acc", bufs=4))
+        ps_tr = ctx.enter_context(tc.psum_pool(name="ps_tr", bufs=4))
+
+        ctx.enter_context(tc.manual_schedule())
+
+        xb = []
+        for n in range(B):
+            xb_n = raw.tile([P, 4, DIM], U8, name="xb%d" % n)
+            xb.append(xb_n)
+        wraw = []
+        for idx in range(16):
+            w_t = raw.tile([P, DIM], BF16, name="wraw%d" % idx)
+            wraw.append(w_t)
+
+        def load_x(n, a):
+            nc.sync.dma_start(out=xb[n][:, a, :], in_=x_bytes[n].rearrange("(p a) k -> p a k", a=4)[:, a, :])
+
+        def load_w(idx):
+            h = idx % 8
+            nc.sync.dma_start(out=wraw[idx][:], in_=weights[idx // 8][h * HD:(h + 1) * HD, :])
+
+        scl = const.tile([P, DIM], F32, name="scl")
+        nc.scalar.dma_start(out=scl[:], in_=x_scale.rearrange("a b k -> (a b k)").partition_broadcast(P))
+        for a in range(4):
+            load_x(0, a)
+        tcol = const.tile([P, 4], F32, name="tcol")
+        nc.gpsimd.iota(tcol[:], pattern=[[1, 4]], base=0, channel_multiplier=4, allow_small_or_imprecise_dtypes=True)
+        braw = const.tile([P, P], BF16, name="braw")
+        nc.gpsimd.memset(braw[:], 0.0)
+        nc.sync.dma_start(out=braw[0:8, :], in_=b_qa.rearrange("(h d) -> h d", d=HD))
+        nc.sync.dma_start(out=braw[8:16, :], in_=b_qt.rearrange("(h d) -> h d", d=HD))
+        for idx in range(6):
+            load_w(idx)
+        for a in range(4):
+            load_x(1, a)
+        for idx in range(6, 16):
+            load_w(idx)
+
+        freq = const.tile([P, 64], F32, name="freq")
+        nc.vector.memset(freq[:, 0:1], -1.0)
+        junk = const.tile([P, 1], F32, name="junk")
+        nc.scalar.activation(out=junk[:], in_=freq[:, 0:1], func=ACT.Sin)
+
+        ident = const.tile([P, P], F32, name="ident")
+        make_identity(nc, ident[:])
+
+        for w in (1, 2, 4, 8, 16, 32):
+            c = ROPE_BASE ** (-w / 64.0)
+            nc.vector.tensor_scalar(out=freq[:, w:2 * w], in0=freq[:, 0:w], scalar1=(-c if w == 1 else c), scalar2=None, op0=ALU.mult)
+        ang = const.tile([P, 256], F32, name="ang")
+        nc.vector.tensor_tensor(out=ang[:].rearrange("p (a j) -> p a j", a=4), in0=freq[:].unsqueeze(1).to_broadcast([P, 4, 64]),
+                                in1=tcol[:].unsqueeze(2).to_broadcast([P, 4, 64]), op=ALU.mult)
+        ki = const.tile([P, 256], I32, name="ki")
+        nc.vector.tensor_scalar(out=ki[:], in0=ang[:], scalar1=1.0 / TWO_PI, scalar2=None, op0=ALU.mult)
+        r1 = const.tile([P, 256], F32, name="r1")
+        nc.vector.scalar_tensor_tensor(out=r1[:], in0=ki[:], scalar=-C1, in1=ang[:], op0=ALU.mult, op1=ALU.add)
+        r4 = const.tile([P, 256], F32, name="r4")
+        nc.vector.scalar_tensor_tensor(out=r4[:], in0=ki[:], scalar=-C2, in1=r1[:], op0=ALU.mult, op1=ALU.add)
+        nabs = const.tile([P, 256], F32, name="nabs")
+        nc.vector.scalar_tensor_tensor(out=nabs[:], in0=r4[:], scalar=-1.0, in1=r4[:], op0=ALU.mult, op1=ALU.min)
+
+        tab2 = const.tile([P, 2, 512], F32, name="tab2")
+        for hf in range(2):
+            nc.scalar.activation(
+                out=tab2[:, 1, :].rearrange("p (a h c e) -> p a h c e", a=4, h=2, e=2)[:, :, hf, :, :],
+                in_=r4[:].rearrange("p (a c e) -> p a c e", a=4, e=2)[:, :, :, ::-1], func=ACT.Sin)
+            nc.scalar.activation(
+                out=tab2[:, 0, :].rearrange("p (a h j) -> p a h j", a=4, h=2)[:, :, hf, :],
+                in_=nabs[:].rearrange("p (a j) -> p a j", a=4), func=ACT.Sin, bias=math.pi / 2.0, scale=1.0)
+
+        swp = const.tile([P, P], F32, name="swp")
+        nc.gpsimd.tensor_copy(out=swp[:].rearrange("p (c e) -> p c e", e=2),
+                              in_=ident[:].rearrange("p (c e) -> p c e", e=2)[:, :, ::-1])
+        tabT = const.tile([P, 2, 512], F32, name="tabT")
+        bf32 = const.tile([P, P], F32, name="bf32")
+        nc.gpsimd.tensor_copy(out=bf32[:], in_=braw[:])
+        bias_f = const.tile([P, 16], F32, name="bias_f")
+        wc = keep.tile([P, 16, 256], U32, name="wc", align_bytes=64)
+        ws = keep.tile([P, 16, 256], U8, name="ws", align_bytes=64)
+        xc = []
+        xs = []
+        xw = []
+        for n in range(B):
+            xc_n = keep.tile([P, 2, 512], U32, name="xc%d" % n, align_bytes=64)
+            xs_n = keep.tile([P, 2, 512], U8, name="xs%d" % n, align_bytes=64)
+            xw_n = keep.tile([P, 4, DIM], BF16, name="xw%d" % n, align_bytes=64)
+            xc.append(xc_n)
+            xs.append(xs_n)
+            xw.append(xw_n)
+        live = {}
+
+        def widen(n, a):
+            nc.vector.tensor_tensor(out=xw[n][:, a, :], in0=xb[n][:, a, :].bitcast(FP8), in1=scl[:], op=ALU.mult)
+
+        def x_turn(n, g, hh):
+            bank = ps_tr.tile([P, 2, 2, P], F32, tag="tr")
+            for u in range(2):
+                for a2 in range(2):
+                    words = xw[n][:, 2 * hh + a2, :].bitcast(F32)
+                    nc.tensor.transpose(bank[:, u, a2, :], words[:, 256 * g + u:256 * (g + 1):2], ident[:])
+            xg = stage.tile([P, 1024], BF16, tag="xgrp", align_bytes=64)
+            nc.scalar.copy(out=xg[:].bitcast(F32).rearrange("p (c u) -> p c u", u=2),
+                           in_=bank[:].rearrange("p u a r -> p (a r) u"))
+            live[("xg", n, g, hh)] = xg
+
+        def x_quant(n, g, hh):
+            cols = slice(256 * hh, 256 * hh + 256)
+            nc.vector.quantize_mx(out=xc[n][:, g, cols].bitcast(FP8X4), scales=xs[n][:, g, cols], in_=live[("xg", n, g, hh)][:])
+
+        def w_turn(idx):
+            if idx % 2 == 0:
+                wg_new = stage.tile([P, 2048], BF16, tag="wgrp", align_bytes=64)
+                live[("wg", idx // 2)] = wg_new
+            wg = live[("wg", idx // 2)]
+            k = idx % 2
+            bank = ps_tr.tile([P, 2, 2, P], F32, tag="tr")
+            words = wraw[idx][:].bitcast(F32)
+            for g in range(2):
+                for u in range(2):
+                    nc.tensor.transpose(bank[:, g, u, :], words[:, 256 * g + u:256 * (g + 1):2], ident[:])
+            nc.scalar.copy(out=wg[:, 1024 * k:1024 * k + 1024].bitcast(F32).rearrange("p (g d u) -> p g d u", g=2, u=2),
+                           in_=bank[:].rearrange("p g u d -> p g d u"))
+
+        def w_quant(pair):
+            nc.vector.quantize_mx(out=wc[:, 2 * pair:2 * pair + 2, :].rearrange("p i c -> p (i c)").bitcast(FP8X4),
+                                  scales=ws[:, 2 * pair:2 * pair + 2, :].rearrange("p i c -> p (i c)"), in_=live[("wg", pair)][:])
+
+        def st_mx(u):
+            n, idx = u // 16, u % 16
+            acc = ps_acc.tile([P, 512], F32, tag="acc")
+            for g in range(2):
+                cols = slice(128 * g, 128 * g + 128)
+                nc.tensor.matmul_mx(out=acc[:], lhsT=wc[:, idx, cols].bitcast(FP8X4), lhsT_scale=ws[:, idx, cols],
+                                    rhs=xc[n][:, g, :].bitcast(FP8X4), rhs_scale=xs[n][:, g, :],
+                                    start=(g == 0), stop=(g == 1))
+            live[("acc", u)] = acc
+
+        def st_bias(u):
+            idx = u % 16
+            qT = epi.tile([P, 512], F32, tag="qT")
+            nc.scalar.activation(out=qT[:], in_=live[("acc", u)][:], func=ACT.Identity, bias=bias_f[:, idx:idx + 1], scale=1.0)
+            live[("qT", u)] = qT
+
+        def st_back(u):
+            qT = live[("qT", u)]
+            tb = ps_tr.tile([P, 512], F32, tag="tr")
+            for a in range(4):
+                nc.tensor.transpose(tb[:, 128 * a:128 * a + 128], qT[:, 128 * a:128 * a + 128], ident[:])
+            live[("tb", u)] = tb
+
+        def st_prod(u):
+            t12 = epi.tile([P, 2, 512], F32, tag="t12")
+            nc.vector.tensor_tensor(out=t12[:], in0=live[("tb", u)][:].unsqueeze(1).to_broadcast([P, 2, 512]), in1=tab2[:], op=ALU.mult)
+            live[("t12", u)] = t12
+
+        def st_add(u):
+            n, idx = u // 16, u % 16
+            t12 = live[("t12", u)]
+            o = epi.tile([P, 512], F32, tag="o")
+            nc.gpsimd.tensor_tensor(out=o[:].rearrange("p (c e) -> p c e", e=2),
+                                    in0=t12[:, 0, :].rearrange("p (c e) -> p c e", e=2),
+                                    in1=t12[:, 1, :].rearrange("p (c e) -> p c e", e=2)[:, :, ::-1], op=ALU.add)
+            nc.sync.dma_start(out=outs[idx // 8][n, idx % 8].rearrange("(p a) d -> p (a d)", a=4), in_=o[:])
+
+        def st_add_v(u):
+            n, idx = u // 16, u % 16
+            t12 = live[("t12", u)]
+            o = epi.tile([P, 512], F32, tag="o")
+            nc.vector.tensor_tensor(out=o[:].rearrange("p (c e) -> p c e", e=2),
+                                    in0=t12[:, 0, :].rearrange("p (c e) -> p c e", e=2),
+                                    in1=t12[:, 1, :].rearrange("p (c e) -> p c e", e=2)[:, :, ::-1], op=ALU.add)
+            nc.sync.dma_start(out=outs[idx // 8][n, idx % 8].rearrange("(p a) d -> p (a d)", a=4), in_=o[:])
+
+        def st_feat_v(u):
+            idx = u % 16
+            ab = epi.tile([P, 2, 512], F32, tag="ab")
+            nc.vector.scalar_tensor_tensor(out=ab[:], in0=live[("acc", u)][:].unsqueeze(1).to_broadcast([P, 2, 512]),
+                                           scalar=bias_f[:, idx:idx + 1], in1=tabT[:], op0=ALU.add, op1=ALU.mult)
+            live[("ab", u)] = ab
+
+        def st_feat_g(u):
+            ab = epi.tile([P, 2, 512], F32, tag="abg")
+            nc.gpsimd.tensor_tensor(out=ab[:], in0=live[("qT", u)][:].unsqueeze(1).to_broadcast([P, 2, 512]), in1=tabT[:], op=ALU.mult)
+            live[("ab", u)] = ab
+
+        def st_back2(u):
+            n, idx = u // 16, u % 16
+            ab = live[("ab", u)]
+            tb = ps_tr.tile([P, 512], F32, tag="tr")
+            for a in range(4):
+                cols = slice(128 * a, 128 * a + 128)
+                nc.tensor.matmul(out=tb[:, cols], lhsT=ab[:, 0, cols], rhs=ident[:], is_transpose=True, start=True, stop=False)
+                nc.tensor.matmul(out=tb[:, cols], lhsT=ab[:, 1, cols], rhs=swp[:], is_transpose=True, start=False, stop=True)
+            o = epi.tile([P, 512], F32, tag="o2")
+            nc.scalar.copy(out=o[:], in_=tb[:])
+            nc.sync.dma_start(out=outs[idx // 8][n, idx % 8].rearrange("(p a) d -> p (a d)", a=4), in_=o[:])
+
+        def kind(u):
+            return KINDS[u] if 0 <= u < 32 else 0
+
+        for a in range(4):
+            widen(0, a)
+        w_turn(0)
+        w_turn(1)
+        x_turn(0, 0, 0)
+        x_turn(0, 1, 0)
+        w_turn(2)
+        w_turn(3)
+        x_turn(0, 0, 1)
+        x_turn(0, 1, 1)
+        bps = ps_tr.tile([P, 512], F32, tag="tr")
+        nc.tensor.transpose(bps[:, 0:P], bf32[:], ident[:])
+        nc.scalar.copy(out=bias_f[:], in_=bps[:, 0:16])
+        w_quant(0)
+        for hh in range(2):
+            for g in range(2):
+                x_quant(0, g, hh)
+        w_turn(4)
+        w_turn(5)
+        for s in range(2):
+            tps = ps_tr.tile([P, 512], F32, tag="tr")
+            for a in range(4):
+                nc.tensor.transpose(tps[:, 128 * a:128 * a + 128], tab2[:, s, 128 * a:128 * a + 128], ident[:])
+            nc.scalar.copy(out=tabT[:, s, :], in_=tps[:])
+        w_quant(1)
+        w_quant(2)
+
+        TURN_W = {0: (6, 7, 8, 9), 1: (10, 11), 2: (12, 13, 14, 15)}
+        TURN_X = {3: ((0, 0), (1, 0), (0, 1), (1, 1))}
+        EXTRA_V = {0: (("w", 0), ("w", 1)), 1: (("qw", 3), ("qw", 4), ("w", 2)), 2: (("w", 3), ("qw", 5)),
+                   3: (("qw", 6), ("qw", 7)), 4: (("qx", 0, 0), ("qx", 1, 0), ("qx", 0, 1), ("qx", 1, 1))}
+        for t in range(13):
+            now = [u for u in (3 * t, 3 * t + 1, 3 * t + 2) if u < 32]
+            for u in now:
+                st_mx(u)
+                if kind(u) != 6:
+                    st_bias(u)
+            for idx in TURN_W.get(t, ()):
+                w_turn(idx)
+            for gh in TURN_X.get(t, ()):
+                x_turn(1, gh[0], gh[1])
+            for u in now:
+                if kind(u) == 1:
+                    st_back(u)
+            for u in (3 * t - 3, 3 * t - 2, 3 * t - 1):
+                if kind(u) == 6:
+                    st_back2(u)
+            for u in (3 * t - 6, 3 * t - 5, 3 * t - 4):
+                if kind(u) == 2:
+                    st_back2(u)
+            for u in now:
+                if kind(u) == 6:
+                    st_feat_v(u)
+            for e in EXTRA_V.get(t, ()):
+                if e[0] == "w":
+                    widen(1, e[1])
+                elif e[0] == "qw":
+                    w_quant(e[1])
+                else:
+                    x_quant(1, e[1], e[2])
+            for u in now:
+                if kind(u) == 2:
+                    st_feat_g(u)
+            for u in now:
+                if kind(u) == 1:
+                    st_prod(u)
+                    if u == 30:
+                        st_add_v(u)
+                    else:
+                        st_add(u)

@@ -22,7 +22,7 @@ FLOPS = 2 * (B * T) * DIM * (2 * NH * HD)
 TWO_PI = 2.0 * math.pi
 C1 = 6.28125
 C2 = TWO_PI - C1
-KINDS = (1, 6, 2) * 10 + (1, 6)
+KINDS = (1, 6, 6) * 10 + (1, 6)
 
 
 def tile_l1regressionmoeactionhead_pa_kernel(tc, x_bytes, x_scale, W_qa, b_qa, W_qt, b_qt, out_0, out_1):

from contextlib import ExitStack
import math

import concourse.mybir as mybir
from concourse.masks import make_identity

F32 = mybir.dt.float32
BF16 = mybir.dt.bfloat16
U8 = mybir.dt.uint8
U32 = mybir.dt.uint32
I32 = mybir.dt.int32
FP8 = mybir.dt.float8_e4m3fn
FP8X4 = mybir.dt.float8_e4m3fn_x4
ALU = mybir.AluOpType
ACT = mybir.ActivationFunctionType

B, T, DIM, NH, HD = 2, 512, 1024, 8, 128
P = 128
ROPE_BASE = 10000.0
FLOPS = 2 * (B * T) * DIM * (2 * NH * HD)

TWO_PI = 2.0 * math.pi
C1 = 6.28125
C2 = TWO_PI - C1
KINDS = (1, 6, 6) * 10 + (1, 6)


def tile_l1regressionmoeactionhead_pa_kernel(tc, x_bytes, x_scale, W_qa, b_qa, W_qt, b_qt, out_0, out_1):
    nc = tc.nc
    outs = (out_0, out_1)
    weights = (W_qa, W_qt)

    with ExitStack() as ctx:
        const = ctx.enter_context(tc.tile_pool(name="const", bufs=1))
        raw = ctx.enter_context(tc.tile_pool(name="raw", bufs=1))
        keep = ctx.enter_context(tc.tile_pool(name="keep", bufs=1))
        stage = ctx.enter_context(tc.tile_pool(name="stage", bufs=8))
        epi = ctx.enter_context(tc.tile_pool(name="epi", bufs=4))
        ps_acc = ctx.enter_context(tc.psum_pool(name="ps_acc", bufs=4))
        ps_tr = ctx.enter_context(tc.psum_pool(name="ps_tr", bufs=4))

        ctx.enter_context(tc.manual_schedule())

        xb = []
        for n in range(B):
            xb_n = raw.tile([P, 4, DIM], U8, name="xb%d" % n)
            xb.append(xb_n)
        wraw = []
        for idx in range(16):
            w_t = raw.tile([P, DIM], BF16, name="wraw%d" % idx)
            wraw.append(w_t)

        def load_x(n, a):
            nc.sync.dma_start(out=xb[n][:, a, :], in_=x_bytes[n].rearrange("(p a) k -> p a k", a=4)[:, a, :])

        def load_w(idx):
            h = idx % 8
            nc.sync.dma_start(out=wraw[idx][:], in_=weights[idx // 8][h * HD:(h + 1) * HD, :])

        scl = const.tile([P, DIM], F32, name="scl")
        nc.scalar.dma_start(out=scl[:], in_=x_scale.rearrange("a b k -> (a b k)").partition_broadcast(P))
        for a in range(4):
            load_x(0, a)
        tcol = const.tile([P, 4], F32, name="tcol")
        nc.gpsimd.iota(tcol[:], pattern=[[1, 4]], base=0, channel_multiplier=4, allow_small_or_imprecise_dtypes=True)
        braw = const.tile([P, P], BF16, name="braw")
        nc.gpsimd.memset(braw[:], 0.0)
        nc.sync.dma_start(out=braw[0:8, :], in_=b_qa.rearrange("(h d) -> h d", d=HD))
        nc.sync.dma_start(out=braw[8:16, :], in_=b_qt.rearrange("(h d) -> h d", d=HD))
        for idx in range(6):
            load_w(idx)
        for a in range(4):
            load_x(1, a)
        for idx in range(6, 16):
            load_w(idx)

        freq = const.tile([P, 64], F32, name="freq")
        nc.vector.memset(freq[:, 0:1], -1.0)
        junk = const.tile([P, 1], F32, name="junk")
        nc.scalar.activation(out=junk[:], in_=freq[:, 0:1], func=ACT.Sin)

        ident = const.tile([P, P], F32, name="ident")
        make_identity(nc, ident[:])

        for w in (1, 2, 4, 8, 16, 32):
            c = ROPE_BASE ** (-w / 64.0)
            nc.vector.tensor_scalar(out=freq[:, w:2 * w], in0=freq[:, 0:w], scalar1=(-c if w == 1 else c), scalar2=None, op0=ALU.mult)
        ang = const.tile([P, 256], F32, name="ang")
        nc.vector.tensor_tensor(out=ang[:].rearrange("p (a j) -> p a j", a=4), in0=freq[:].unsqueeze(1).to_broadcast([P, 4, 64]),
                                in1=tcol[:].unsqueeze(2).to_broadcast([P, 4, 64]), op=ALU.mult)
        ki = const.tile([P, 256], I32, name="ki")
        nc.vector.tensor_scalar(out=ki[:], in0=ang[:], scalar1=1.0 / TWO_PI, scalar2=None, op0=ALU.mult)
        r1 = const.tile([P, 256], F32, name="r1")
        nc.vector.scalar_tensor_tensor(out=r1[:], in0=ki[:], scalar=-C1, in1=ang[:], op0=ALU.mult, op1=ALU.add)
        r4 = const.tile([P, 256], F32, name="r4")
        nc.vector.scalar_tensor_tensor(out=r4[:], in0=ki[:], scalar=-C2, in1=r1[:], op0=ALU.mult, op1=ALU.add)
        nabs = const.tile([P, 256], F32, name="nabs")
        nc.vector.scalar_tensor_tensor(out=nabs[:], in0=r4[:], scalar=-1.0, in1=r4[:], op0=ALU.mult, op1=ALU.min)

        tab2 = const.tile([P, 2, 512], F32, name="tab2")
        for hf in range(2):
            nc.scalar.activation(
                out=tab2[:, 1, :].rearrange("p (a h c e) -> p a h c e", a=4, h=2, e=2)[:, :, hf, :, :],
                in_=r4[:].rearrange("p (a c e) -> p a c e", a=4, e=2)[:, :, :, ::-1], func=ACT.Sin)
            nc.scalar.activation(
                out=tab2[:, 0, :].rearrange("p (a h j) -> p a h j", a=4, h=2)[:, :, hf, :],
                in_=nabs[:].rearrange("p (a j) -> p a j", a=4), func=ACT.Sin, bias=math.pi / 2.0, scale=1.0)

        swp = const.tile([P, P], F32, name="swp")
        nc.gpsimd.tensor_copy(out=swp[:].rearrange("p (c e) -> p c e", e=2),
                              in_=ident[:].rearrange("p (c e) -> p c e", e=2)[:, :, ::-1])
        tabT = const.tile([P, 2, 512], F32, name="tabT")
        bf32 = const.tile([P, P], F32, name="bf32")
        nc.gpsimd.tensor_copy(out=bf32[:], in_=braw[:])
        bias_f = const.tile([P, 16], F32, name="bias_f")
        wc = keep.tile([P, 16, 256], U32, name="wc", align_bytes=64)
        ws = keep.tile([P, 16, 256], U8, name="ws", align_bytes=64)
        xc = []
        xs = []
        xw = []
        for n in range(B):
            xc_n = keep.tile([P, 2, 512], U32, name="xc%d" % n, align_bytes=64)
            xs_n = keep.tile([P, 2, 512], U8, name="xs%d" % n, align_bytes=64)
            xw_n = keep.tile([P, 4, DIM], BF16, name="xw%d" % n, align_bytes=64)
            xc.append(xc_n)
            xs.append(xs_n)
            xw.append(xw_n)
        live = {}

        def widen(n, a):
            nc.vector.tensor_tensor(out=xw[n][:, a, :], in0=xb[n][:, a, :].bitcast(FP8), in1=scl[:], op=ALU.mult)

        def x_turn(n, g, hh):
            bank = ps_tr.tile([P, 2, 2, P], F32, tag="tr")
            for u in range(2):
                for a2 in range(2):
                    words = xw[n][:, 2 * hh + a2, :].bitcast(F32)
                    nc.tensor.transpose(bank[:, u, a2, :], words[:, 256 * g + u:256 * (g + 1):2], ident[:])
            xg = stage.tile([P, 1024], BF16, tag="xgrp", align_bytes=64)
            nc.scalar.copy(out=xg[:].bitcast(F32).rearrange("p (c u) -> p c u", u=2),
                           in_=bank[:].rearrange("p u a r -> p (a r) u"))
            live[("xg", n, g, hh)] = xg

        def x_quant(n, g, hh):
            cols = slice(256 * hh, 256 * hh + 256)
            nc.vector.quantize_mx(out=xc[n][:, g, cols].bitcast(FP8X4), scales=xs[n][:, g, cols], in_=live[("xg", n, g, hh)][:])

        def w_turn(idx):
            if idx % 2 == 0:
                wg_new = stage.tile([P, 2048], BF16, tag="wgrp", align_bytes=64)
                live[("wg", idx // 2)] = wg_new
            wg = live[("wg", idx // 2)]
            k = idx % 2
            bank = ps_tr.tile([P, 2, 2, P], F32, tag="tr")
            words = wraw[idx][:].bitcast(F32)
            for g in range(2):
                for u in range(2):
                    nc.tensor.transpose(bank[:, g, u, :], words[:, 256 * g + u:256 * (g + 1):2], ident[:])
            nc.scalar.copy(out=wg[:, 1024 * k:1024 * k + 1024].bitcast(F32).rearrange("p (g d u) -> p g d u", g=2, u=2),
                           in_=bank[:].rearrange("p g u d -> p g d u"))

        def w_quant(pair):
            nc.vector.quantize_mx(out=wc[:, 2 * pair:2 * pair + 2, :].rearrange("p i c -> p (i c)").bitcast(FP8X4),
                                  scales=ws[:, 2 * pair:2 * pair + 2, :].rearrange("p i c -> p (i c)"), in_=live[("wg", pair)][:])

        def st_mx(u):
            n, idx = u // 16, u % 16
            acc = ps_acc.tile([P, 512], F32, tag="acc")
            for g in range(2):
                cols = slice(128 * g, 128 * g + 128)
                nc.tensor.matmul_mx(out=acc[:], lhsT=wc[:, idx, cols].bitcast(FP8X4), lhsT_scale=ws[:, idx, cols],
                                    rhs=xc[n][:, g, :].bitcast(FP8X4), rhs_scale=xs[n][:, g, :],
                                    start=(g == 0), stop=(g == 1))
            live[("acc", u)] = acc

        def st_bias(u):
            idx = u % 16
            qT = epi.tile([P, 512], F32, tag="qT")
            nc.scalar.activation(out=qT[:], in_=live[("acc", u)][:], func=ACT.Identity, bias=bias_f[:, idx:idx + 1], scale=1.0)
            live[("qT", u)] = qT

        def st_back(u):
            qT = live[("qT", u)]
            tb = ps_tr.tile([P, 512], F32, tag="tr")
            for a in range(4):
                nc.tensor.transpose(tb[:, 128 * a:128 * a + 128], qT[:, 128 * a:128 * a + 128], ident[:])
            live[("tb", u)] = tb

        def st_prod(u):
            t12 = epi.tile([P, 2, 512], F32, tag="t12")
            nc.vector.tensor_tensor(out=t12[:], in0=live[("tb", u)][:].unsqueeze(1).to_broadcast([P, 2, 512]), in1=tab2[:], op=ALU.mult)
            live[("t12", u)] = t12

        def st_add(u):
            n, idx = u // 16, u % 16
            t12 = live[("t12", u)]
            o = epi.tile([P, 512], F32, tag="o")
            nc.gpsimd.tensor_tensor(out=o[:].rearrange("p (c e) -> p c e", e=2),
                                    in0=t12[:, 0, :].rearrange("p (c e) -> p c e", e=2),
                                    in1=t12[:, 1, :].rearrange("p (c e) -> p c e", e=2)[:, :, ::-1], op=ALU.add)
            nc.sync.dma_start(out=outs[idx // 8][n, idx % 8].rearrange("(p a) d -> p (a d)", a=4), in_=o[:])

        def st_add_v(u):
            n, idx = u // 16, u % 16
            t12 = live[("t12", u)]
            o = epi.tile([P, 512], F32, tag="o")
            nc.vector.tensor_tensor(out=o[:].rearrange("p (c e) -> p c e", e=2),
                                    in0=t12[:, 0, :].rearrange("p (c e) -> p c e", e=2),
                                    in1=t12[:, 1, :].rearrange("p (c e) -> p c e", e=2)[:, :, ::-1], op=ALU.add)
            nc.sync.dma_start(out=outs[idx // 8][n, idx % 8].rearrange("(p a) d -> p (a d)", a=4), in_=o[:])

        def st_feat_v(u):
            idx = u % 16
            ab = epi.tile([P, 2, 512], F32, tag="ab")
            nc.vector.scalar_tensor_tensor(out=ab[:], in0=live[("acc", u)][:].unsqueeze(1).to_broadcast([P, 2, 512]),
                                           scalar=bias_f[:, idx:idx + 1], in1=tabT[:], op0=ALU.add, op1=ALU.mult)
            live[("ab", u)] = ab

        def st_feat_g(u):
            ab = epi.tile([P, 2, 512], F32, tag="abg")
            nc.gpsimd.tensor_tensor(out=ab[:], in0=live[("qT", u)][:].unsqueeze(1).to_broadcast([P, 2, 512]), in1=tabT[:], op=ALU.mult)
            live[("ab", u)] = ab

        def st_back2(u):
            n, idx = u // 16, u % 16
            ab = live[("ab", u)]
            tb = ps_tr.tile([P, 512], F32, tag="tr")
            for a in range(4):
                cols = slice(128 * a, 128 * a + 128)
                nc.tensor.matmul(out=tb[:, cols], lhsT=ab[:, 0, cols], rhs=ident[:], is_transpose=True, start=True, stop=False)
                nc.tensor.matmul(out=tb[:, cols], lhsT=ab[:, 1, cols], rhs=swp[:], is_transpose=True, start=False, stop=True)
            o = epi.tile([P, 512], F32, tag="o2")
            nc.scalar.copy(out=o[:], in_=tb[:])
            nc.sync.dma_start(out=outs[idx // 8][n, idx % 8].rearrange("(p a) d -> p (a d)", a=4), in_=o[:])

        def kind(u):
            return KINDS[u] if 0 <= u < 32 else 0

        for a in range(4):
            widen(0, a)
        w_turn(0)
        w_turn(1)
        x_turn(0, 0, 0)
        x_turn(0, 1, 0)
        w_turn(2)
        w_turn(3)
        x_turn(0, 0, 1)
        x_turn(0, 1, 1)
        bps = ps_tr.tile([P, 512], F32, tag="tr")
        nc.tensor.transpose(bps[:, 0:P], bf32[:], ident[:])
        nc.scalar.copy(out=bias_f[:], in_=bps[:, 0:16])
        w_quant(0)
        for hh in range(2):
            for g in range(2):
                x_quant(0, g, hh)
        w_turn(4)
        w_turn(5)
        for s in range(2):
            tps = ps_tr.tile([P, 512], F32, tag="tr")
            for a in range(4):
                nc.tensor.transpose(tps[:, 128 * a:128 * a + 128], tab2[:, s, 128 * a:128 * a + 128], ident[:])
            nc.scalar.copy(out=tabT[:, s, :], in_=tps[:])
        w_quant(1)
        w_quant(2)

        TURN_W = {0: (6, 7, 8, 9), 1: (10, 11), 2: (12, 13, 14, 15)}
        TURN_X = {3: ((0, 0), (1, 0), (0, 1), (1, 1))}
        EXTRA_V = {0: (("w", 0), ("w", 1)), 1: (("qw", 3), ("qw", 4), ("w", 2)), 2: (("w", 3), ("qw", 5)),
                   3: (("qw", 6), ("qw", 7)), 4: (("qx", 0, 0), ("qx", 1, 0), ("qx", 0, 1), ("qx", 1, 1))}
        for t in range(13):
            now = [u for u in (3 * t, 3 * t + 1, 3 * t + 2) if u < 32]
            for u in now:
                st_mx(u)
                if kind(u) != 6:
                    st_bias(u)
            for idx in TURN_W.get(t, ()):
                w_turn(idx)
            for gh in TURN_X.get(t, ()):
                x_turn(1, gh[0], gh[1])
            for u in now:
                if kind(u) == 1:
                    st_back(u)
            for u in (3 * t - 3, 3 * t - 2, 3 * t - 1):
                if kind(u) == 6:
                    st_back2(u)
            for u in (3 * t - 6, 3 * t - 5, 3 * t - 4):
                if kind(u) == 2:
                    st_back2(u)
            for u in now:
                if kind(u) == 6:
                    st_feat_v(u)
            for e in EXTRA_V.get(t, ()):
                if e[0] == "w":
                    widen(1, e[1])
                elif e[0] == "qw":
                    w_quant(e[1])
                else:
                    x_quant(1, e[1], e[2])
            for u in now:
                if kind(u) == 2:
                    st_feat_g(u)
            for u in now:
                if kind(u) == 1:
                    st_prod(u)
                    if u == 30:
                        st_add_v(u)
                    else:
                        st_add(u)
